import numpy as np
import ml_dtypes


def mxq(x, axis, fmt="e4m3"):
    dtype, down = {"e4m3": (ml_dtypes.float8_e4m3fn, 7), "e5m2": (ml_dtypes.float8_e5m2, 14)}[fmt]
    v = np.moveaxis(np.asarray(x, np.float32).astype(ml_dtypes.bfloat16).astype(np.float64), axis, -1)
    blocks = v.reshape(v.shape[:-1] + (-1, 32))
    amax = np.abs(blocks).max(-1, keepdims=True)
    byte = np.maximum(np.where(amax > 0, np.frexp(amax)[1] - 1 + 127, 0) - down, 1)
    scale = np.exp2(byte - 127.0)
    codes = (blocks / scale).astype(np.float32).astype(dtype).astype(np.float64)
    return np.moveaxis((codes * scale).reshape(v.shape), -1, axis)


WIDE = False


def mx_kscale(k):
    if not WIDE:
        return np.ones(k)
    levels = np.array([10, -10, 5, -5, 0])
    a = np.random.permutation(np.resize(levels, k // 512 * 4)).reshape(k // 512, 4)
    idx = np.arange(k)
    return np.exp2(a[idx // 512, idx % 128 // 32])


BF16 = ml_dtypes.bfloat16


def bf(x):
    return np.asarray(x, np.float32).astype(BF16)


def f64(x):
    return np.asarray(x).astype(np.float64)


E2M1 = np.array([0.0, 0.5, 1.0, 1.5, 2.0, 3.0, 4.0, 6.0, -0.0, -0.5, -1.0, -1.5, -2.0, -3.0, -4.0, -6.0])


def pack_weight(w, fmt):
    k, n = w.shape
    w = f64(bf(w)).reshape(k // 32, 32, n)
    amax = np.abs(w).max(1)
    if fmt == "e4m3":
        byte = np.frexp(amax)[1] - 1 + 127 - 7
    else:
        mant, ex = np.frexp(amax / 6.0)
        byte = np.where(mant > 0.5, ex, ex - 1) + 127
    byte = np.clip(np.where(amax > 0, byte, 1), 1, 254)
    scaled = (w * np.exp2(127.0 - byte)[:, None, :]).reshape(k, n).astype(np.float32)
    by_word = np.ascontiguousarray(scaled.reshape(k // 512, 128, 4, n).transpose(0, 1, 3, 2))
    if fmt == "e4m3":
        words = by_word.astype(ml_dtypes.float8_e4m3fn).view(np.uint8)
    else:
        c = by_word.astype(ml_dtypes.float4_e2m1fn).view(np.uint8) & 0xF
        words = c[..., 0::2] | (c[..., 1::2] << 4)
    return np.ascontiguousarray(words), np.ascontiguousarray(byte.astype(np.uint8).reshape(k // 512, 16, n))


def unpack_weight(words, scales, fmt):
    g, p, n, _ = words.shape
    if fmt == "e4m3":
        vals = np.ascontiguousarray(words).view(ml_dtypes.float8_e4m3fn).astype(np.float64)
    else:
        nib = np.empty((g, p, n, 4), np.uint8)
        nib[..., 0::2] = words & 0xF
        nib[..., 1::2] = words >> 4
        vals = E2M1[nib]
    vals = vals * np.repeat(np.exp2(scales.astype(np.float64) - 127.0), 8, axis=1)[..., None]
    return vals.transpose(0, 1, 3, 2).reshape(g * 512, n)

def pack4(w):
    words, scales = pack_weight(w, "e2m1")
    return words.reshape(words.shape[0], 128, -1), scales


def unpack4(words, scales):
    return unpack_weight(words.reshape(words.shape[0], 128, -1, 2), scales, "e2m1")


B, C, H, W, M, O = 5, 512, 16, 16, 512, 512
N = B * H * W
L2_EPS = 1e-12
BN_EPS = 1e-5


def l2_normalize(x, axis):
    n = np.sqrt(np.sum(x * x, axis=axis, keepdims=True))
    return x / np.maximum(n, L2_EPS)


def setup_inputs():
    s = mx_kscale(C)
    cm = (np.random.standard_normal((N, C)) * 5.0 + np.random.standard_normal((1, C)) * 1.5) / np.sqrt(C)
    w = np.random.standard_normal((O, 2 * C)) * 0.1 / np.sqrt(2 * C)
    w[:, C:] = w[:, C:] / s
    words, scales = pack4(np.ascontiguousarray(w.T))
    return {"query": bf(np.random.standard_normal((B, C, H, W))), "concat_memory": bf(cm * s),
            "conv_w_words": words, "conv_w_scales": scales,
            "bn_gamma": bf(1.0 + 0.1 * np.random.standard_normal(O)), "bn_beta": bf(0.2 * np.random.standard_normal(O))}


def reference(query, concat_memory, conv_w_words, conv_w_scales, bn_gamma, bn_beta):
    q_flat = l2_normalize(f64(query), 1).transpose(0, 2, 3, 1).reshape(N, C)
    upd = np.concatenate([q_flat, f64(concat_memory)], axis=1)
    y = mxq(upd, 1, "e4m3") @ unpack4(conv_w_words, conv_w_scales)
    y = y.reshape(B, H, W, O).transpose(0, 3, 1, 2)
    mean = np.mean(y, axis=(0, 2, 3), keepdims=True)
    var = np.mean((y - mean) ** 2, axis=(0, 2, 3), keepdims=True)
    y = (y - mean) / np.sqrt(var + BN_EPS)
    y = y * f64(bn_gamma)[None, :, None, None] + f64(bn_beta)[None, :, None, None]
    return np.maximum(y, 0.0)

@@ -1,0 +1,250 @@
+from contextlib import ExitStack
+
+import concourse.mybir as mybir
+from concourse.masks import make_identity
+
+F32 = mybir.dt.float32
+BF16 = mybir.dt.bfloat16
+I32 = mybir.dt.int32
+U32 = mybir.dt.uint32
+U8 = mybir.dt.uint8
+FP8X4 = mybir.dt.float8_e4m3fn_x4
+FP4X4 = mybir.dt.float4_e2m1fn_x4
+ACT = mybir.ActivationFunctionType
+ALU = mybir.AluOpType
+
+P = 128
+PACK = 4
+BATCH = 5
+CHANNELS = 512
+HW = 256
+PIXELS = BATCH * HW
+OUT_CHANNELS = 512
+OUT_TILES = OUT_CHANNELS // P
+PASSES = 2
+HALVES = HW // P
+BANK = 512
+L2_EPS = 1e-12
+BN_EPS = 1e-5
+BN_STATS_DIM = 6
+BN_AGGR_DIM = 2
+
+FLOPS = 2 * PIXELS * PASSES * CHANNELS * OUT_CHANNELS
+
+
+def tile_memory_sup_pb_kernel(
+    tc, query, concat_memory, conv_w_words, conv_w_scales, bn_gamma, bn_beta, out
+):
+    nc = tc.nc
+    with ExitStack() as ctx:
+        keep = ctx.enter_context(tc.tile_pool(name="keep", bufs=1))
+        stage = ctx.enter_context(tc.tile_pool(name="stage", bufs=3))
+
+        gain_shift_rows = keep.tile([P, P], BF16)
+        nc.vector.memset(gain_shift_rows[:], 0.0)
+        nc.scalar.dma_start(
+            out=gain_shift_rows[0:OUT_TILES, :], in_=bn_gamma.rearrange("(j p) -> j p", p=P)
+        )
+        nc.scalar.dma_start(
+            out=gain_shift_rows[OUT_TILES : 2 * OUT_TILES, :],
+            in_=bn_beta.rearrange("(j p) -> j p", p=P),
+        )
+
+        tiny = keep.tile([P, 1], F32)
+        nc.vector.memset(tiny[:], 1e-30)
+        bn_eps = keep.tile([P, 1], F32)
+        nc.vector.memset(bn_eps[:], BN_EPS)
+        table_warm = keep.tile([P, 1], F32)
+        nc.scalar.activation(out=table_warm[:], in_=bn_eps[:], func=ACT.Abs_reciprocal_sqrt)
+
+        ident_bf = keep.tile([P, P], BF16)
+        make_identity(nc, ident_bf[:])
+        ident_f32 = keep.tile([P, P], F32)
+        make_identity(nc, ident_f32[:])
+
+        w_scales = keep.tile([P, PASSES, OUT_CHANNELS], U8, align_bytes=64)
+        nc.vector.memset(w_scales[:].bitcast(I32), 0)
+
+        q_sb = keep.tile([P, BATCH, PACK, HW], BF16)
+        cm_sb = keep.tile([P, BATCH, HALVES, CHANNELS], BF16)
+
+        def load_q(b):
+            nc.sync.dma_start(
+                out=q_sb[:, b], in_=query[b].rearrange("(p t) h w -> p t (h w)", t=PACK)
+            )
+
+        def load_cm(c):
+            nc.sync.dma_start(
+                out=cm_sb[:, c],
+                in_=concat_memory[HW * c : HW * (c + 1), :].rearrange(
+                    "(r j) k -> r j k", j=HALVES
+                ),
+            )
+
+        for b in range(BATCH):
+            load_q(b)
+            load_cm(b)
+
+        w_words = keep.tile([P, PASSES, 2 * OUT_CHANNELS], U8, align_bytes=64)
+        nc.sync.dma_start(
+            out=w_words[:].bitcast(I32),
+            in_=conv_w_words.bitcast(I32).rearrange("g p n -> p g n"),
+        )
+        for quadrant in range(4):
+            nc.sync.dma_start(
+                out=w_scales[32 * quadrant : 32 * quadrant + 4].bitcast(I32),
+                in_=conv_w_scales.bitcast(I32)[:, 4 * quadrant : 4 * quadrant + 4, :].rearrange(
+                    "g r n -> r g n"
+                ),
+            )
+        upd_codes = keep.tile([P, PASSES, PIXELS], U32, align_bytes=64)
+        upd_scales = keep.tile([P, PASSES, PIXELS], U8, align_bytes=64)
+
+        squares = keep.tile([P, BATCH * HALVES, CHANNELS], BF16)
+        sum_sq = keep.tile([P, BATCH * HALVES], F32)
+        inv_norm = keep.tile([P, BATCH * HALVES], F32)
+        gain_shift = keep.tile([P, 2 * OUT_TILES], F32)
+
+        with tc.psum_pool(name="prep", bufs=1) as prep:
+
+            def norms(b):
+                for h in range(HALVES):
+                    j = HALVES * b + h
+                    q_t = prep.tile([P, PACK, P], BF16, tag="q_t", bufs=3)
+                    for t in range(PACK):
+                        nc.tensor.transpose(
+                            q_t[:, t, :], q_sb[:, b, t, P * h : P * (h + 1)], ident_bf[:]
+                        )
+                    nc.scalar.activation(
+                        out=squares[:, j, :],
+                        in_=q_t[:].rearrange("n t p -> n (t p)"),
+                        func=ACT.Square,
+                        accum_out=sum_sq[:, j : j + 1],
+                    )
+                tiles_b = slice(HALVES * b, HALVES * (b + 1))
+                nc.scalar.activation(
+                    out=inv_norm[:, tiles_b],
+                    in_=sum_sq[:, tiles_b],
+                    func=ACT.Abs_reciprocal_sqrt,
+                    bias=tiny[:],
+                )
+
+            def normalise(b):
+                inv_norm_all = prep.tile([P, HW], F32, tag="inv_norm_all", bufs=2)
+                for h in range(HALVES):
+                    j = HALVES * b + h
+                    nc.tensor.matmul(
+                        inv_norm_all[:, P * h : P * (h + 1)],
+                        lhsT=inv_norm[:, j : j + 1].to_broadcast([P, P]),
+                        rhs=ident_f32[:],
+                        start=True,
+                        stop=True,
+                    )
+                q_grouped = stage.tile([P, HW, PACK], BF16, align_bytes=64)
+                nc.vector.scalar_tensor_tensor(
+                    out=q_grouped[:],
+                    in0=inv_norm_all[:].unsqueeze(2).to_broadcast([P, HW, PACK]),
+                    scalar=1.0 / L2_EPS,
+                    in1=q_sb[:, b].rearrange("p t n -> p n t"),
+                    op0=ALU.min,
+                    op1=ALU.mult,
+                )
+                return q_grouped
+
+            def memory_words(c):
+                cm_t = prep.tile([P, HALVES, 2, P], F32, tag="cm_t", bufs=2)
+                for j in range(HALVES):
+                    cm_words = cm_sb[:, c, j, :].bitcast(F32)
+                    for u in range(2):
+                        nc.tensor.transpose(
+                            cm_t[:, j, u, :], cm_words[:, u : CHANNELS // 2 : 2], ident_f32[:]
+                        )
+                cm_grouped = stage.tile([P, HW * 2], F32, align_bytes=64)
+                nc.scalar.copy(
+                    out=cm_grouped[:].rearrange("p (r j u) -> p r j u", j=HALVES, u=2),
+                    in_=cm_t[:].rearrange("p j u r -> p r j u"),
+                )
+                return cm_grouped
+
+            def quantise(g, c, grouped_bf16):
+                cols = slice(HW * c, HW * (c + 1))
+                nc.vector.quantize_mx(
+                    out=upd_codes[:, g, cols].bitcast(FP8X4),
+                    scales=upd_scales[:, g, cols],
+                    in_=grouped_bf16,
+                )
+
+            norms(0)
+            cm_grouped = memory_words(0)
+            gain_shift_t = prep.tile([P, P], BF16, tag="gain_shift_t", bufs=1)
+            nc.tensor.transpose(gain_shift_t[:], gain_shift_rows[:], ident_bf[:])
+            nc.vector.tensor_copy(out=gain_shift[:], in_=gain_shift_t[:, 0 : 2 * OUT_TILES])
+            for b in range(BATCH):
+                if b + 1 < BATCH:
+                    norms(b + 1)
+                q_grouped = normalise(b)
+                quantise(1, b, cm_grouped[:].bitcast(BF16))
+                if b + 1 < BATCH:
+                    cm_grouped = memory_words(b + 1)
+                quantise(0, b, q_grouped[:].rearrange("p n t -> p (n t)"))
+
+        stats = keep.tile([P, OUT_TILES, 3, BN_STATS_DIM], F32)
+        mean_var = keep.tile([P, OUT_TILES, BN_AGGR_DIM], F32)
+        inv_std = keep.tile([P, OUT_TILES], F32)
+        scale = keep.tile([P, OUT_TILES], F32)
+        mean_scaled = keep.tile([P, OUT_TILES], F32)
+        shift = keep.tile([P, OUT_TILES], F32)
+        out_view = out.rearrange("b (o p) h w -> o p b (h w)", p=P)
+
+        bank_starts = range(0, PIXELS, BANK)
+
+        with tc.psum_pool(name="acc", bufs=8, reuse_waits="tile") as acc:
+            for o in range(OUT_TILES):
+                y_banks = []
+                for i, first in enumerate(bank_starts):
+                    width = min(BANK, PIXELS - first)
+                    n_pass = BANK if width == BANK else P
+                    y = acc.tile([P, BANK], F32, tag="y")
+                    y_banks.append(y)
+                    for n0 in range(0, width, n_pass):
+                        cols = slice(first + n0, first + n0 + n_pass)
+                        for g in range(PASSES):
+                            nc.tensor.matmul_mx(
+                                out=y[:, n0 : n0 + n_pass],
+                                lhsT=w_words[:, g, 2 * P * o : 2 * P * (o + 1)].bitcast(FP4X4),
+                                lhsT_scale=w_scales[:, g, P * o : P * (o + 1)],
+                                rhs=upd_codes[:, g, cols].bitcast(FP8X4),
+                                rhs_scale=upd_scales[:, g, cols],
+                                start=(g == 0),
+                                stop=(g == PASSES - 1),
+                            )
+                    nc.vector.bn_stats(out=stats[:, o, i, :], in_=y[:, 0:width])
+                nc.vector.bn_aggr(
+                    out=mean_var[:, o, :], in_=stats[:, o].rearrange("p i s -> p (i s)")
+                )
+                one = slice(o, o + 1)
+                nc.scalar.activation(
+                    out=inv_std[:, one],
+                    in_=mean_var[:, o, 1:2],
+                    func=ACT.Abs_reciprocal_sqrt,
+                    bias=bn_eps[:],
+                )
+                nc.vector.tensor_mul(scale[:, one], gain_shift[:, one], inv_std[:, one])
+                nc.vector.tensor_mul(mean_scaled[:, one], mean_var[:, o, 0:1], scale[:, one])
+                nc.vector.tensor_sub(
+                    shift[:, one], gain_shift[:, OUT_TILES + o : OUT_TILES + o + 1], mean_scaled[:, one]
+                )
+                result = stage.tile([P, PIXELS], F32, bufs=OUT_TILES)
+                for i, first in enumerate(bank_starts):
+                    width = min(BANK, PIXELS - first)
+                    nc.scalar.activation(
+                        out=result[:, first : first + width],
+                        in_=y_banks[i][:, 0:width],
+                        func=ACT.Relu,
+                        scale=scale[:, one],
+                        bias=shift[:, one],
+                    )
+                    nc.sync.dma_start(
+                        out=out_view[o][:, first // HW : (first + width) // HW, :],
+                        in_=result[:, first : first + width].rearrange("p (b n) -> p b n", n=HW),
+                    )

@@ -24,10 +24,12 @@ OUT_TILES = OUT_CHANNELS // P
 PASSES = 2
 HALVES = HW // P
 BANK = 512
+BANK_STARTS = tuple(range(0, PIXELS, BANK))
 L2_EPS = 1e-12
 BN_EPS = 1e-5
 BN_STATS_DIM = 6
 BN_AGGR_DIM = 2
+CM_CHUNKS_ON_VECTOR = 3
 
 FLOPS = 2 * PIXELS * PASSES * CHANNELS * OUT_CHANNELS
 
@@ -37,6 +39,7 @@ def tile_memory_sup_pb_kernel(
 ):
     nc = tc.nc
     with ExitStack() as ctx:
+        ctx.enter_context(tc.manual_schedule())
         keep = ctx.enter_context(tc.tile_pool(name="keep", bufs=1))
         stage = ctx.enter_context(tc.tile_pool(name="stage", bufs=3))
 
@@ -50,12 +53,12 @@ def tile_memory_sup_pb_kernel(
             in_=bn_beta.rearrange("(j p) -> j p", p=P),
         )
 
-        tiny = keep.tile([P, 1], F32)
-        nc.vector.memset(tiny[:], 1e-30)
-        bn_eps = keep.tile([P, 1], F32)
-        nc.vector.memset(bn_eps[:], BN_EPS)
+        neg_half = keep.tile([P, HALVES], F32)
+        nc.vector.memset(neg_half[:], -0.5)
         table_warm = keep.tile([P, 1], F32)
-        nc.scalar.activation(out=table_warm[:], in_=bn_eps[:], func=ACT.Abs_reciprocal_sqrt)
+        nc.scalar.activation(
+            out=table_warm[:], in_=neg_half[:, 0:1], func=ACT.Abs_reciprocal_sqrt
+        )
 
         ident_bf = keep.tile([P, P], BF16)
         make_identity(nc, ident_bf[:])
@@ -67,24 +70,16 @@ def tile_memory_sup_pb_kernel(
 
         q_sb = keep.tile([P, BATCH, PACK, HW], BF16)
         cm_sb = keep.tile([P, BATCH, HALVES, CHANNELS], BF16)
-
-        def load_q(b):
+        for b in range(BATCH):
             nc.sync.dma_start(
                 out=q_sb[:, b], in_=query[b].rearrange("(p t) h w -> p t (h w)", t=PACK)
             )
-
-        def load_cm(c):
             nc.sync.dma_start(
-                out=cm_sb[:, c],
-                in_=concat_memory[HW * c : HW * (c + 1), :].rearrange(
+                out=cm_sb[:, b],
+                in_=concat_memory[HW * b : HW * (b + 1), :].rearrange(
                     "(r j) k -> r j k", j=HALVES
                 ),
             )
-
-        for b in range(BATCH):
-            load_q(b)
-            load_cm(b)
-
         w_words = keep.tile([P, PASSES, 2 * OUT_CHANNELS], U8, align_bytes=64)
         nc.sync.dma_start(
             out=w_words[:].bitcast(I32),
@@ -97,20 +92,23 @@ def tile_memory_sup_pb_kernel(
                     "g r n -> r g n"
                 ),
             )
+
         upd_codes = keep.tile([P, PASSES, PIXELS], U32, align_bytes=64)
         upd_scales = keep.tile([P, PASSES, PIXELS], U8, align_bytes=64)
 
         squares = keep.tile([P, BATCH * HALVES, CHANNELS], BF16)
         sum_sq = keep.tile([P, BATCH * HALVES], F32)
+        sum_clamped = keep.tile([P, BATCH * HALVES], F32)
         inv_norm = keep.tile([P, BATCH * HALVES], F32)
         gain_shift = keep.tile([P, 2 * OUT_TILES], F32)
+        neg_gain = keep.tile([P, OUT_TILES], F32)
 
         with tc.psum_pool(name="prep", bufs=1) as prep:
 
             def norms(b):
                 for h in range(HALVES):
                     j = HALVES * b + h
-                    q_t = prep.tile([P, PACK, P], BF16, tag="q_t", bufs=3)
+                    q_t = prep.tile([P, PACK, P], BF16, tag="q_t", bufs=4)
                     for t in range(PACK):
                         nc.tensor.transpose(
                             q_t[:, t, :], q_sb[:, b, t, P * h : P * (h + 1)], ident_bf[:]
@@ -122,11 +120,14 @@ def tile_memory_sup_pb_kernel(
                         accum_out=sum_sq[:, j : j + 1],
                     )
                 tiles_b = slice(HALVES * b, HALVES * (b + 1))
-                nc.scalar.activation(
+                nc.gpsimd.tensor_scalar_max(
+                    sum_clamped[:, tiles_b], sum_sq[:, tiles_b], L2_EPS * L2_EPS
+                )
+                nc.gpsimd.tensor_tensor(
                     out=inv_norm[:, tiles_b],
-                    in_=sum_sq[:, tiles_b],
-                    func=ACT.Abs_reciprocal_sqrt,
-                    bias=tiny[:],
+                    in0=sum_clamped[:, tiles_b],
+                    in1=neg_half[:],
+                    op=ALU.pow,
                 )
 
             def normalise(b):
@@ -141,15 +142,12 @@ def tile_memory_sup_pb_kernel(
                         stop=True,
                     )
                 q_grouped = stage.tile([P, HW, PACK], BF16, align_bytes=64)
-                nc.vector.scalar_tensor_tensor(
-                    out=q_grouped[:],
-                    in0=inv_norm_all[:].unsqueeze(2).to_broadcast([P, HW, PACK]),
-                    scalar=1.0 / L2_EPS,
-                    in1=q_sb[:, b].rearrange("p t n -> p n t"),
-                    op0=ALU.min,
-                    op1=ALU.mult,
+                nc.vector.tensor_mul(
+                    q_grouped[:],
+                    inv_norm_all[:].unsqueeze(2).to_broadcast([P, HW, PACK]),
+                    q_sb[:, b].rearrange("p t n -> p n t"),
                 )
-                return q_grouped
+                return q_grouped[:].rearrange("p n t -> p (n t)")
 
             def memory_words(c):
                 cm_t = prep.tile([P, HALVES, 2, P], F32, tag="cm_t", bufs=2)
@@ -160,48 +158,52 @@ def tile_memory_sup_pb_kernel(
                             cm_t[:, j, u, :], cm_words[:, u : CHANNELS // 2 : 2], ident_f32[:]
                         )
                 cm_grouped = stage.tile([P, HW * 2], F32, align_bytes=64)
-                nc.scalar.copy(
-                    out=cm_grouped[:].rearrange("p (r j u) -> p r j u", j=HALVES, u=2),
-                    in_=cm_t[:].rearrange("p j u r -> p r j u"),
-                )
-                return cm_grouped
+                side_by_side = cm_grouped[:].rearrange("p (r j u) -> p r j u", j=HALVES, u=2)
+                if c < CM_CHUNKS_ON_VECTOR:
+                    nc.vector.tensor_copy(out=side_by_side, in_=cm_t[:].rearrange("p j u r -> p r j u"))
+                else:
+                    nc.scalar.copy(out=side_by_side, in_=cm_t[:].rearrange("p j u r -> p r j u"))
+                return cm_grouped[:].bitcast(BF16)
 
-            def quantise(g, c, grouped_bf16):
+            def quantise(g, c, grouped):
                 cols = slice(HW * c, HW * (c + 1))
                 nc.vector.quantize_mx(
                     out=upd_codes[:, g, cols].bitcast(FP8X4),
                     scales=upd_scales[:, g, cols],
-                    in_=grouped_bf16,
+                    in_=grouped,
                 )
 
-            norms(0)
-            cm_grouped = memory_words(0)
-            gain_shift_t = prep.tile([P, P], BF16, tag="gain_shift_t", bufs=1)
+            cm_grouped = {}
+            q_grouped = {}
+            for step in range(BATCH + 3):
+                if step < BATCH:
+                    norms(step)
+                    cm_grouped[step] = memory_words(step)
+                if 0 <= step - 1 < BATCH:
+                    quantise(1, step - 1, cm_grouped[step - 1])
+                if 0 <= step - 2 < BATCH:
+                    q_grouped[step - 2] = normalise(step - 2)
+                if 0 <= step - 3 < BATCH:
+                    quantise(0, step - 3, q_grouped[step - 3])
+
+            gain_shift_t = prep.tile([P, P], BF16, tag="cm_t", bufs=2)
             nc.tensor.transpose(gain_shift_t[:], gain_shift_rows[:], ident_bf[:])
             nc.vector.tensor_copy(out=gain_shift[:], in_=gain_shift_t[:, 0 : 2 * OUT_TILES])
-            for b in range(BATCH):
-                if b + 1 < BATCH:
-                    norms(b + 1)
-                q_grouped = normalise(b)
-                quantise(1, b, cm_grouped[:].bitcast(BF16))
-                if b + 1 < BATCH:
-                    cm_grouped = memory_words(b + 1)
-                quantise(0, b, q_grouped[:].rearrange("p n t -> p (n t)"))
+            nc.vector.tensor_scalar_mul(neg_gain[:], gain_shift[:, 0:OUT_TILES], -1.0)
 
-        stats = keep.tile([P, OUT_TILES, 3, BN_STATS_DIM], F32)
+        stats = keep.tile([P, OUT_TILES, len(BANK_STARTS), BN_STATS_DIM], F32)
         mean_var = keep.tile([P, OUT_TILES, BN_AGGR_DIM], F32)
+        neg_gain_mean = keep.tile([P, OUT_TILES], F32)
         inv_std = keep.tile([P, OUT_TILES], F32)
         scale = keep.tile([P, OUT_TILES], F32)
-        mean_scaled = keep.tile([P, OUT_TILES], F32)
         shift = keep.tile([P, OUT_TILES], F32)
         out_view = out.rearrange("b (o p) h w -> o p b (h w)", p=P)
 
-        bank_starts = range(0, PIXELS, BANK)
-
         with tc.psum_pool(name="acc", bufs=8, reuse_waits="tile") as acc:
-            for o in range(OUT_TILES):
+
+            def statistics(o):
                 y_banks = []
-                for i, first in enumerate(bank_starts):
+                for i, first in enumerate(BANK_STARTS):
                     width = min(BANK, PIXELS - first)
                     n_pass = BANK if width == BANK else P
                     y = acc.tile([P, BANK], F32, tag="y")
@@ -222,29 +224,56 @@ def tile_memory_sup_pb_kernel(
                 nc.vector.bn_aggr(
                     out=mean_var[:, o, :], in_=stats[:, o].rearrange("p i s -> p (i s)")
                 )
+                nc.vector.tensor_mul(
+                    neg_gain_mean[:, o : o + 1], mean_var[:, o, 0:1], neg_gain[:, o : o + 1]
+                )
+                return y_banks
+
+            def finish(o, y_banks):
                 one = slice(o, o + 1)
                 nc.scalar.activation(
                     out=inv_std[:, one],
                     in_=mean_var[:, o, 1:2],
                     func=ACT.Abs_reciprocal_sqrt,
-                    bias=bn_eps[:],
+                    bias=BN_EPS,
                 )
-                nc.vector.tensor_mul(scale[:, one], gain_shift[:, one], inv_std[:, one])
-                nc.vector.tensor_mul(mean_scaled[:, one], mean_var[:, o, 0:1], scale[:, one])
-                nc.vector.tensor_sub(
-                    shift[:, one], gain_shift[:, OUT_TILES + o : OUT_TILES + o + 1], mean_scaled[:, one]
+                nc.scalar.activation(
+                    out=scale[:, one], in_=gain_shift[:, one], func=ACT.Copy, scale=inv_std[:, one]
+                )
+                nc.scalar.activation(
+                    out=shift[:, one],
+                    in_=neg_gain_mean[:, one],
+                    func=ACT.Identity,
+                    scale=inv_std[:, one],
+                    bias=gain_shift[:, OUT_TILES + o : OUT_TILES + o + 1],
                 )
                 result = stage.tile([P, PIXELS], F32, bufs=OUT_TILES)
-                for i, first in enumerate(bank_starts):
+                for i, first in enumerate(BANK_STARTS):
                     width = min(BANK, PIXELS - first)
-                    nc.scalar.activation(
-                        out=result[:, first : first + width],
-                        in_=y_banks[i][:, 0:width],
-                        func=ACT.Relu,
-                        scale=scale[:, one],
-                        bias=shift[:, one],
-                    )
+                    y = y_banks[i][:, 0:width]
+                    res = result[:, first : first + width]
+                    if o >= OUT_TILES - 2 and i == 1:
+                        nc.vector.tensor_scalar(
+                            out=res,
+                            in0=y,
+                            scalar1=scale[:, one],
+                            scalar2=shift[:, one],
+                            op0=ALU.mult,
+                            op1=ALU.add,
+                        )
+                        nc.vector.tensor_scalar_max(res, res, 0.0)
+                    else:
+                        nc.scalar.activation(
+                            out=res, in_=y, func=ACT.Relu, scale=scale[:, one], bias=shift[:, one]
+                        )
                     nc.sync.dma_start(
                         out=out_view[o][:, first // HW : (first + width) // HW, :],
-                        in_=result[:, first : first + width].rearrange("p (b n) -> p b n", n=HW),
+                        in_=res.rearrange("p (b n) -> p b n", n=HW),
                     )
+
+            y_of = {}
+            for o in range(OUT_TILES + 1):
+                if o < OUT_TILES:
+                    y_of[o] = statistics(o)
+                if o > 0:
+                    finish(o - 1, y_of[o - 1])

@@ -23,6 +23,7 @@ OUT_CHANNELS = 512
 OUT_TILES = OUT_CHANNELS // P
 PASSES = 2
 HALVES = HW // P
+PAIR = 2
 BANK = 512
 BANK_STARTS = tuple(range(0, PIXELS, BANK))
 L2_EPS = 1e-12
@@ -53,7 +54,7 @@ def tile_memory_sup_pb_kernel(
             in_=bn_beta.rearrange("(j p) -> j p", p=P),
         )
 
-        neg_half = keep.tile([P, HALVES], F32)
+        neg_half = keep.tile([P, PAIR], F32)
         nc.vector.memset(neg_half[:], -0.5)
         table_warm = keep.tile([P, 1], F32)
         nc.scalar.activation(
@@ -96,46 +97,40 @@ def tile_memory_sup_pb_kernel(
         upd_codes = keep.tile([P, PASSES, PIXELS], U32, align_bytes=64)
         upd_scales = keep.tile([P, PASSES, PIXELS], U8, align_bytes=64)
 
-        squares = keep.tile([P, BATCH * HALVES, CHANNELS], BF16)
-        sum_sq = keep.tile([P, BATCH * HALVES], F32)
-        sum_clamped = keep.tile([P, BATCH * HALVES], F32)
-        inv_norm = keep.tile([P, BATCH * HALVES], F32)
+        squares = keep.tile([P, BATCH * PAIR, CHANNELS], BF16)
+        sum_sq = keep.tile([P, BATCH * PAIR], F32)
+        sum_clamped = keep.tile([P, BATCH * PAIR], F32)
+        inv_norm = keep.tile([P, BATCH * PAIR], F32)
         gain_shift = keep.tile([P, 2 * OUT_TILES], F32)
         neg_gain = keep.tile([P, OUT_TILES], F32)
 
         with tc.psum_pool(name="prep", bufs=1) as prep:
 
             def norms(b):
-                for h in range(HALVES):
-                    j = HALVES * b + h
-                    q_t = prep.tile([P, PACK, P], BF16, tag="q_t", bufs=4)
-                    for t in range(PACK):
-                        nc.tensor.transpose(
-                            q_t[:, t, :], q_sb[:, b, t, P * h : P * (h + 1)], ident_bf[:]
-                        )
+                q_t = prep.tile([P, PACK, P], F32, tag="q_t", bufs=4)
+                for t in range(PACK):
+                    nc.tensor.transpose(q_t[:, t, :], q_sb[:, b, t, :].bitcast(F32), ident_f32[:])
+                pixel_pairs = q_t[:].rearrange("w t p -> w (t p)").bitcast(BF16)
+                for e in range(PAIR):
+                    j = PAIR * b + e
                     nc.scalar.activation(
                         out=squares[:, j, :],
-                        in_=q_t[:].rearrange("n t p -> n (t p)"),
+                        in_=pixel_pairs[:, e : PAIR * CHANNELS : PAIR],
                         func=ACT.Square,
                         accum_out=sum_sq[:, j : j + 1],
                     )
-                tiles_b = slice(HALVES * b, HALVES * (b + 1))
-                nc.gpsimd.tensor_scalar_max(
-                    sum_clamped[:, tiles_b], sum_sq[:, tiles_b], L2_EPS * L2_EPS
-                )
+                both = slice(PAIR * b, PAIR * (b + 1))
+                nc.gpsimd.tensor_scalar_max(sum_clamped[:, both], sum_sq[:, both], L2_EPS * L2_EPS)
                 nc.gpsimd.tensor_tensor(
-                    out=inv_norm[:, tiles_b],
-                    in0=sum_clamped[:, tiles_b],
-                    in1=neg_half[:],
-                    op=ALU.pow,
+                    out=inv_norm[:, both], in0=sum_clamped[:, both], in1=neg_half[:], op=ALU.pow
                 )
 
             def normalise(b):
-                inv_norm_all = prep.tile([P, HW], F32, tag="inv_norm_all", bufs=2)
-                for h in range(HALVES):
-                    j = HALVES * b + h
+                inv_norm_all = prep.tile([P, PAIR, P], F32, tag="inv_norm_all", bufs=2)
+                for e in range(PAIR):
+                    j = PAIR * b + e
                     nc.tensor.matmul(
-                        inv_norm_all[:, P * h : P * (h + 1)],
+                        inv_norm_all[:, e, :],
                         lhsT=inv_norm[:, j : j + 1].to_broadcast([P, P]),
                         rhs=ident_f32[:],
                         start=True,
@@ -143,9 +138,12 @@ def tile_memory_sup_pb_kernel(
                     )
                 q_grouped = stage.tile([P, HW, PACK], BF16, align_bytes=64)
                 nc.vector.tensor_mul(
-                    q_grouped[:],
-                    inv_norm_all[:].unsqueeze(2).to_broadcast([P, HW, PACK]),
-                    q_sb[:, b].rearrange("p t n -> p n t"),
+                    q_grouped[:].rearrange("p (w e) t -> p w e t", e=PAIR),
+                    inv_norm_all[:]
+                    .rearrange("p e w -> p w e")
+                    .unsqueeze(3)
+                    .to_broadcast([P, P, PAIR, PACK]),
+                    q_sb[:, b].rearrange("p t (w e) -> p w e t", e=PAIR),
                 )
                 return q_grouped[:].rearrange("p n t -> p (n t)")
 
@@ -175,12 +173,18 @@ def tile_memory_sup_pb_kernel(
 
             cm_grouped = {}
             q_grouped = {}
+            cm_step = [
+                c if c < CM_CHUNKS_ON_VECTOR else c + BATCH - CM_CHUNKS_ON_VECTOR
+                for c in range(BATCH)
+            ]
             for step in range(BATCH + 3):
                 if step < BATCH:
                     norms(step)
-                    cm_grouped[step] = memory_words(step)
-                if 0 <= step - 1 < BATCH:
-                    quantise(1, step - 1, cm_grouped[step - 1])
+                for c in range(BATCH):
+                    if cm_step[c] == step:
+                        cm_grouped[c] = memory_words(c)
+                    if cm_step[c] == step - 1:
+                        quantise(1, c, cm_grouped[c])
                 if 0 <= step - 2 < BATCH:
                     q_grouped[step - 2] = normalise(step - 2)
                 if 0 <= step - 3 < BATCH:
@@ -188,8 +192,8 @@ def tile_memory_sup_pb_kernel(
 
             gain_shift_t = prep.tile([P, P], BF16, tag="cm_t", bufs=2)
             nc.tensor.transpose(gain_shift_t[:], gain_shift_rows[:], ident_bf[:])
-            nc.vector.tensor_copy(out=gain_shift[:], in_=gain_shift_t[:, 0 : 2 * OUT_TILES])
-            nc.vector.tensor_scalar_mul(neg_gain[:], gain_shift[:, 0:OUT_TILES], -1.0)
+            nc.scalar.copy(out=gain_shift[:], in_=gain_shift_t[:, 0 : 2 * OUT_TILES])
+            nc.scalar.mul(neg_gain[:], gain_shift_t[:, 0:OUT_TILES], -1.0)
 
         stats = keep.tile([P, OUT_TILES, len(BANK_STARTS), BN_STATS_DIM], F32)
         mean_var = keep.tile([P, OUT_TILES, BN_AGGR_DIM], F32)

@@ -23,14 +23,13 @@ OUT_CHANNELS = 512
 OUT_TILES = OUT_CHANNELS // P
 PASSES = 2
 HALVES = HW // P
-PAIR = 2
 BANK = 512
 BANK_STARTS = tuple(range(0, PIXELS, BANK))
 L2_EPS = 1e-12
 BN_EPS = 1e-5
 BN_STATS_DIM = 6
 BN_AGGR_DIM = 2
-CM_CHUNKS_ON_VECTOR = 3
+CM_CHUNKS_ON_VECTOR = 2
 
 FLOPS = 2 * PIXELS * PASSES * CHANNELS * OUT_CHANNELS
 
@@ -54,7 +53,7 @@ def tile_memory_sup_pb_kernel(
             in_=bn_beta.rearrange("(j p) -> j p", p=P),
         )
 
-        neg_half = keep.tile([P, PAIR], F32)
+        neg_half = keep.tile([P, HALVES], F32)
         nc.vector.memset(neg_half[:], -0.5)
         table_warm = keep.tile([P, 1], F32)
         nc.scalar.activation(
@@ -97,40 +96,46 @@ def tile_memory_sup_pb_kernel(
         upd_codes = keep.tile([P, PASSES, PIXELS], U32, align_bytes=64)
         upd_scales = keep.tile([P, PASSES, PIXELS], U8, align_bytes=64)
 
-        squares = keep.tile([P, BATCH * PAIR, CHANNELS], BF16)
-        sum_sq = keep.tile([P, BATCH * PAIR], F32)
-        sum_clamped = keep.tile([P, BATCH * PAIR], F32)
-        inv_norm = keep.tile([P, BATCH * PAIR], F32)
+        squares = keep.tile([P, BATCH * HALVES, CHANNELS], BF16)
+        sum_sq = keep.tile([P, BATCH * HALVES], F32)
+        sum_clamped = keep.tile([P, BATCH * HALVES], F32)
+        inv_norm = keep.tile([P, BATCH * HALVES], F32)
         gain_shift = keep.tile([P, 2 * OUT_TILES], F32)
         neg_gain = keep.tile([P, OUT_TILES], F32)
 
         with tc.psum_pool(name="prep", bufs=1) as prep:
 
             def norms(b):
-                q_t = prep.tile([P, PACK, P], F32, tag="q_t", bufs=4)
-                for t in range(PACK):
-                    nc.tensor.transpose(q_t[:, t, :], q_sb[:, b, t, :].bitcast(F32), ident_f32[:])
-                pixel_pairs = q_t[:].rearrange("w t p -> w (t p)").bitcast(BF16)
-                for e in range(PAIR):
-                    j = PAIR * b + e
+                for h in range(HALVES):
+                    j = HALVES * b + h
+                    q_t = prep.tile([P, PACK, P], BF16, tag="q_t", bufs=4)
+                    for t in range(PACK):
+                        nc.tensor.transpose(
+                            q_t[:, t, :], q_sb[:, b, t, P * h : P * (h + 1)], ident_bf[:]
+                        )
                     nc.scalar.activation(
                         out=squares[:, j, :],
-                        in_=pixel_pairs[:, e : PAIR * CHANNELS : PAIR],
+                        in_=q_t[:].rearrange("n t p -> n (t p)"),
                         func=ACT.Square,
                         accum_out=sum_sq[:, j : j + 1],
                     )
-                both = slice(PAIR * b, PAIR * (b + 1))
-                nc.gpsimd.tensor_scalar_max(sum_clamped[:, both], sum_sq[:, both], L2_EPS * L2_EPS)
+                tiles_b = slice(HALVES * b, HALVES * (b + 1))
+                nc.gpsimd.tensor_scalar_max(
+                    sum_clamped[:, tiles_b], sum_sq[:, tiles_b], L2_EPS * L2_EPS
+                )
                 nc.gpsimd.tensor_tensor(
-                    out=inv_norm[:, both], in0=sum_clamped[:, both], in1=neg_half[:], op=ALU.pow
+                    out=inv_norm[:, tiles_b],
+                    in0=sum_clamped[:, tiles_b],
+                    in1=neg_half[:],
+                    op=ALU.pow,
                 )
 
             def normalise(b):
-                inv_norm_all = prep.tile([P, PAIR, P], F32, tag="inv_norm_all", bufs=2)
-                for e in range(PAIR):
-                    j = PAIR * b + e
+                inv_norm_all = prep.tile([P, HW], F32, tag="inv_norm_all", bufs=2)
+                for h in range(HALVES):
+                    j = HALVES * b + h
                     nc.tensor.matmul(
-                        inv_norm_all[:, e, :],
+                        inv_norm_all[:, P * h : P * (h + 1)],
                         lhsT=inv_norm[:, j : j + 1].to_broadcast([P, P]),
                         rhs=ident_f32[:],
                         start=True,
@@ -138,12 +143,9 @@ def tile_memory_sup_pb_kernel(
                     )
                 q_grouped = stage.tile([P, HW, PACK], BF16, align_bytes=64)
                 nc.vector.tensor_mul(
-                    q_grouped[:].rearrange("p (w e) t -> p w e t", e=PAIR),
-                    inv_norm_all[:]
-                    .rearrange("p e w -> p w e")
-                    .unsqueeze(3)
-                    .to_broadcast([P, P, PAIR, PACK]),
-                    q_sb[:, b].rearrange("p t (w e) -> p w e t", e=PAIR),
+                    q_grouped[:],
+                    inv_norm_all[:].unsqueeze(2).to_broadcast([P, HW, PACK]),
+                    q_sb[:, b].rearrange("p t n -> p n t"),
                 )
                 return q_grouped[:].rearrange("p n t -> p (n t)")
 
@@ -177,7 +179,7 @@ def tile_memory_sup_pb_kernel(
                 c if c < CM_CHUNKS_ON_VECTOR else c + BATCH - CM_CHUNKS_ON_VECTOR
                 for c in range(BATCH)
             ]
-            for step in range(BATCH + 3):
+            for step in range(max(BATCH + 3, cm_step[BATCH - 1] + 2)):
                 if step < BATCH:
                     norms(step)
                 for c in range(BATCH):
@@ -228,7 +230,7 @@ def tile_memory_sup_pb_kernel(
                 nc.vector.bn_aggr(
                     out=mean_var[:, o, :], in_=stats[:, o].rearrange("p i s -> p (i s)")
                 )
-                nc.vector.tensor_mul(
+                nc.gpsimd.tensor_mul(
                     neg_gain_mean[:, o : o + 1], mean_var[:, o, 0:1], neg_gain[:, o : o + 1]
                 )
                 return y_banks

@@ -134,12 +134,10 @@ def tile_memory_sup_pb_kernel(
                 inv_norm_all = prep.tile([P, HW], F32, tag="inv_norm_all", bufs=2)
                 for h in range(HALVES):
                     j = HALVES * b + h
-                    nc.tensor.matmul(
+                    nc.tensor.transpose(
                         inv_norm_all[:, P * h : P * (h + 1)],
-                        lhsT=inv_norm[:, j : j + 1].to_broadcast([P, P]),
-                        rhs=ident_f32[:],
-                        start=True,
-                        stop=True,
+                        inv_norm[:, j : j + 1].to_broadcast([P, P]),
+                        ident_f32[:],
                     )
                 q_grouped = stage.tile([P, HW, PACK], BF16, align_bytes=64)
                 nc.vector.tensor_mul(

@@ -30,6 +30,7 @@ BN_EPS = 1e-5
 BN_STATS_DIM = 6
 BN_AGGR_DIM = 2
 CM_CHUNKS_ON_VECTOR = 2
+WARM_UP_WIDTHS = (HW, P)
 
 FLOPS = 2 * PIXELS * PASSES * CHANNELS * OUT_CHANNELS
 
@@ -43,15 +44,10 @@ def tile_memory_sup_pb_kernel(
         keep = ctx.enter_context(tc.tile_pool(name="keep", bufs=1))
         stage = ctx.enter_context(tc.tile_pool(name="stage", bufs=3))
 
+        zeros = keep.tile([P, HW], F32)
+        nc.vector.memset(zeros[:], 0.0)
         gain_shift_rows = keep.tile([P, P], BF16)
         nc.vector.memset(gain_shift_rows[:], 0.0)
-        nc.scalar.dma_start(
-            out=gain_shift_rows[0:OUT_TILES, :], in_=bn_gamma.rearrange("(j p) -> j p", p=P)
-        )
-        nc.scalar.dma_start(
-            out=gain_shift_rows[OUT_TILES : 2 * OUT_TILES, :],
-            in_=bn_beta.rearrange("(j p) -> j p", p=P),
-        )
 
         neg_half = keep.tile([P, HALVES], F32)
         nc.vector.memset(neg_half[:], -0.5)
@@ -92,6 +88,14 @@ def tile_memory_sup_pb_kernel(
                     "g r n -> r g n"
                 ),
             )
+
+        nc.sync.dma_start(
+            out=gain_shift_rows[0:OUT_TILES, :], in_=bn_gamma.rearrange("(j p) -> j p", p=P)
+        )
+        nc.sync.dma_start(
+            out=gain_shift_rows[OUT_TILES : 2 * OUT_TILES, :],
+            in_=bn_beta.rearrange("(j p) -> j p", p=P),
+        )
 
         upd_codes = keep.tile([P, PASSES, PIXELS], U32, align_bytes=64)
         upd_scales = keep.tile([P, PASSES, PIXELS], U8, align_bytes=64)
@@ -169,6 +173,12 @@ def tile_memory_sup_pb_kernel(
                     out=upd_codes[:, g, cols].bitcast(FP8X4),
                     scales=upd_scales[:, g, cols],
                     in_=grouped,
+                )
+
+            warm = prep.tile([P, HW], F32, tag="inv_norm_all", bufs=2)
+            for width in WARM_UP_WIDTHS:
+                nc.tensor.matmul(
+                    warm[:, 0:width], lhsT=zeros[:, 0:P], rhs=zeros[:, 0:width], start=True, stop=True
                 )
 
             cm_grouped = {}

@@ -29,8 +29,7 @@ L2_EPS = 1e-12
 BN_EPS = 1e-5
 BN_STATS_DIM = 6
 BN_AGGR_DIM = 2
-CM_CHUNKS_ON_VECTOR = 2
-WARM_UP_WIDTHS = (HW, P)
+CM_CHUNKS_ON_VECTOR = 1
 
 FLOPS = 2 * PIXELS * PASSES * CHANNELS * OUT_CHANNELS
 
@@ -44,20 +43,22 @@ def tile_memory_sup_pb_kernel(
         keep = ctx.enter_context(tc.tile_pool(name="keep", bufs=1))
         stage = ctx.enter_context(tc.tile_pool(name="stage", bufs=3))
 
-        zeros = keep.tile([P, HW], F32)
-        nc.vector.memset(zeros[:], 0.0)
         gain_shift_rows = keep.tile([P, P], BF16)
         nc.vector.memset(gain_shift_rows[:], 0.0)
 
-        neg_half = keep.tile([P, HALVES], F32)
-        nc.vector.memset(neg_half[:], -0.5)
+        one_column = keep.tile([P, 1], F32)
+        nc.vector.memset(one_column[:], 1.0)
         table_warm = keep.tile([P, 1], F32)
         nc.scalar.activation(
-            out=table_warm[:], in_=neg_half[:, 0:1], func=ACT.Abs_reciprocal_sqrt
+            out=table_warm[:], in_=one_column[:], func=ACT.Abs_reciprocal_sqrt
         )
 
         ident_bf = keep.tile([P, P], BF16)
         make_identity(nc, ident_bf[:])
+        beside = keep.tile([P, P], BF16)
+        nc.gpsimd.tensor_scalar(
+            out=beside[:], in0=ident_bf[:], scalar1=-1.0, scalar2=2.0**120, op0=ALU.add, op1=ALU.mult
+        )
         ident_f32 = keep.tile([P, P], F32)
         make_identity(nc, ident_f32[:])
 
@@ -66,16 +67,29 @@ def tile_memory_sup_pb_kernel(
 
         q_sb = keep.tile([P, BATCH, PACK, HW], BF16)
         cm_sb = keep.tile([P, BATCH, HALVES, CHANNELS], BF16)
-        for b in range(BATCH):
+
+        def load_query(b):
             nc.sync.dma_start(
                 out=q_sb[:, b], in_=query[b].rearrange("(p t) h w -> p t (h w)", t=PACK)
             )
+
+        def load_memory(c):
             nc.sync.dma_start(
-                out=cm_sb[:, b],
-                in_=concat_memory[HW * b : HW * (b + 1), :].rearrange(
+                out=cm_sb[:, c],
+                in_=concat_memory[HW * c : HW * (c + 1), :].rearrange(
                     "(r j) k -> r j k", j=HALVES
                 ),
             )
+
+        load_query(0)
+        load_memory(0)
+        load_query(1)
+        load_query(2)
+        load_memory(1)
+        load_query(3)
+        load_query(4)
+        for c in range(2, BATCH):
+            load_memory(c)
         w_words = keep.tile([P, PASSES, 2 * OUT_CHANNELS], U8, align_bytes=64)
         nc.sync.dma_start(
             out=w_words[:].bitcast(I32),
@@ -102,12 +116,20 @@ def tile_memory_sup_pb_kernel(
 
         squares = keep.tile([P, BATCH * HALVES, CHANNELS], BF16)
         sum_sq = keep.tile([P, BATCH * HALVES], F32)
-        sum_clamped = keep.tile([P, BATCH * HALVES], F32)
         inv_norm = keep.tile([P, BATCH * HALVES], F32)
         gain_shift = keep.tile([P, 2 * OUT_TILES], F32)
         neg_gain = keep.tile([P, OUT_TILES], F32)
 
         with tc.psum_pool(name="prep", bufs=1) as prep:
+
+            def inverse_norms(b):
+                tiles_b = slice(HALVES * b, HALVES * (b + 1))
+                nc.scalar.activation(
+                    out=inv_norm[:, tiles_b],
+                    in_=sum_sq[:, tiles_b],
+                    func=ACT.Abs_reciprocal_sqrt,
+                    bias=L2_EPS * L2_EPS,
+                )
 
             def norms(b):
                 for h in range(HALVES):
@@ -124,15 +146,13 @@ def tile_memory_sup_pb_kernel(
                         accum_out=sum_sq[:, j : j + 1],
                     )
                 tiles_b = slice(HALVES * b, HALVES * (b + 1))
-                nc.gpsimd.tensor_scalar_max(
-                    sum_clamped[:, tiles_b], sum_sq[:, tiles_b], L2_EPS * L2_EPS
+                nc.scalar.activation(
+                    out=sum_sq[:, tiles_b],
+                    in_=sum_sq[:, tiles_b],
+                    func=ACT.Relu,
+                    bias=-L2_EPS * L2_EPS,
                 )
-                nc.gpsimd.tensor_tensor(
-                    out=inv_norm[:, tiles_b],
-                    in0=sum_clamped[:, tiles_b],
-                    in1=neg_half[:],
-                    op=ALU.pow,
-                )
+                inverse_norms(b)
 
             def normalise(b):
                 inv_norm_all = prep.tile([P, HW], F32, tag="inv_norm_all", bufs=2)
@@ -175,32 +195,53 @@ def tile_memory_sup_pb_kernel(
                     in_=grouped,
                 )
 
-            warm = prep.tile([P, HW], F32, tag="inv_norm_all", bufs=2)
-            for width in WARM_UP_WIDTHS:
-                nc.tensor.matmul(
-                    warm[:, 0:width], lhsT=zeros[:, 0:P], rhs=zeros[:, 0:width], start=True, stop=True
-                )
+            def product_norms(b):
+                for h in range(HALVES):
+                    j = HALVES * b + h
+                    gram = prep.tile([P, P], F32, tag="q_t", bufs=4)
+                    for t in range(PACK):
+                        pixels = q_sb[:, b, t, P * h : P * (h + 1)]
+                        nc.tensor.matmul(gram[:], lhsT=pixels, rhs=pixels, start=(t == 0), stop=False)
+                    nc.tensor.matmul(
+                        gram[:], lhsT=ident_bf[:], rhs=beside[:], start=False, stop=True
+                    )
+                    nc.scalar.activation(
+                        out=squares[:, j, 0:P],
+                        in_=gram[:],
+                        func=ACT.Relu,
+                        bias=-L2_EPS * L2_EPS,
+                        accum_out=sum_sq[:, j : j + 1],
+                    )
+                inverse_norms(b)
 
-            cm_grouped = {}
-            q_grouped = {}
-            cm_step = [
-                c if c < CM_CHUNKS_ON_VECTOR else c + BATCH - CM_CHUNKS_ON_VECTOR
-                for c in range(BATCH)
-            ]
-            for step in range(max(BATCH + 3, cm_step[BATCH - 1] + 2)):
-                if step < BATCH:
-                    norms(step)
-                for c in range(BATCH):
-                    if cm_step[c] == step:
-                        cm_grouped[c] = memory_words(c)
-                    if cm_step[c] == step - 1:
-                        quantise(1, c, cm_grouped[c])
-                if 0 <= step - 2 < BATCH:
-                    q_grouped[step - 2] = normalise(step - 2)
-                if 0 <= step - 3 < BATCH:
-                    quantise(0, step - 3, q_grouped[step - 3])
 
-            gain_shift_t = prep.tile([P, P], BF16, tag="cm_t", bufs=2)
+            product_norms(0)
+            m0 = memory_words(0)
+            product_norms(1)
+            quantise(1, 0, m0)
+            q0 = normalise(0)
+            product_norms(2)
+            q1 = normalise(1)
+            norms(3)
+            quantise(0, 0, q0)
+            m1 = memory_words(1)
+            q2 = normalise(2)
+            quantise(0, 1, q1)
+            norms(4)
+            quantise(1, 1, m1)
+            q3 = normalise(3)
+            m2 = memory_words(2)
+            quantise(0, 2, q2)
+            m3 = memory_words(3)
+            q4 = normalise(4)
+            quantise(0, 3, q3)
+            quantise(1, 2, m2)
+            m4 = memory_words(4)
+            quantise(0, 4, q4)
+            quantise(1, 3, m3)
+            quantise(1, 4, m4)
+
+            gain_shift_t = prep.tile([P, P], BF16, tag="q_t", bufs=4)
             nc.tensor.transpose(gain_shift_t[:], gain_shift_rows[:], ident_bf[:])
             nc.scalar.copy(out=gain_shift[:], in_=gain_shift_t[:, 0 : 2 * OUT_TILES])
             nc.scalar.mul(neg_gain[:], gain_shift_t[:, 0:OUT_TILES], -1.0)

@@ -29,6 +29,10 @@ L2_EPS = 1e-12
 BN_EPS = 1e-5
 BN_STATS_DIM = 6
 BN_AGGR_DIM = 2
+TRIPLE = BN_STATS_DIM // 2
+BANK_ORDER = ((0, 0), (0, 1), (0, 2), (1, 0), (1, 1), (1, 2), (2, 0), (2, 1))
+SCALAR_STATS = ((0, 0),)
+VECTOR_FINISHES = ((2, 1), (3, 1))
 CM_CHUNKS_ON_VECTOR = 1
 
 FLOPS = 2 * PIXELS * PASSES * CHANNELS * OUT_CHANNELS
@@ -45,6 +49,13 @@ def tile_memory_sup_pb_kernel(
 
         gain_shift_rows = keep.tile([P, P], BF16)
         nc.vector.memset(gain_shift_rows[:], 0.0)
+        nc.scalar.dma_start(
+            out=gain_shift_rows[0:OUT_TILES, :], in_=bn_gamma.rearrange("(j p) -> j p", p=P)
+        )
+        nc.scalar.dma_start(
+            out=gain_shift_rows[OUT_TILES : 2 * OUT_TILES, :],
+            in_=bn_beta.rearrange("(j p) -> j p", p=P),
+        )
 
         one_column = keep.tile([P, 1], F32)
         nc.vector.memset(one_column[:], 1.0)
@@ -102,14 +113,6 @@ def tile_memory_sup_pb_kernel(
                     "g r n -> r g n"
                 ),
             )
-
-        nc.sync.dma_start(
-            out=gain_shift_rows[0:OUT_TILES, :], in_=bn_gamma.rearrange("(j p) -> j p", p=P)
-        )
-        nc.sync.dma_start(
-            out=gain_shift_rows[OUT_TILES : 2 * OUT_TILES, :],
-            in_=bn_beta.rearrange("(j p) -> j p", p=P),
-        )
 
         upd_codes = keep.tile([P, PASSES, PIXELS], U32, align_bytes=64)
         upd_scales = keep.tile([P, PASSES, PIXELS], U8, align_bytes=64)
@@ -187,6 +190,12 @@ def tile_memory_sup_pb_kernel(
                     nc.scalar.copy(out=side_by_side, in_=cm_t[:].rearrange("p j u r -> p r j u"))
                 return cm_grouped[:].bitcast(BF16)
 
+            def gains():
+                gain_shift_t = prep.tile([P, P], BF16, tag="q_t", bufs=4)
+                nc.tensor.transpose(gain_shift_t[:], gain_shift_rows[:], ident_bf[:])
+                nc.scalar.copy(out=gain_shift[:], in_=gain_shift_t[:, 0 : 2 * OUT_TILES])
+                nc.scalar.mul(neg_gain[:], gain_shift_t[:, 0:OUT_TILES], -1.0)
+
             def quantise(g, c, grouped):
                 cols = slice(HW * c, HW * (c + 1))
                 nc.vector.quantize_mx(
@@ -233,20 +242,18 @@ def tile_memory_sup_pb_kernel(
             m2 = memory_words(2)
             quantise(0, 2, q2)
             m3 = memory_words(3)
+            gains()
             q4 = normalise(4)
             quantise(0, 3, q3)
             quantise(1, 2, m2)
             m4 = memory_words(4)
-            quantise(0, 4, q4)
             quantise(1, 3, m3)
+            quantise(0, 4, q4)
             quantise(1, 4, m4)
 
-            gain_shift_t = prep.tile([P, P], BF16, tag="q_t", bufs=4)
-            nc.tensor.transpose(gain_shift_t[:], gain_shift_rows[:], ident_bf[:])
-            nc.scalar.copy(out=gain_shift[:], in_=gain_shift_t[:, 0 : 2 * OUT_TILES])
-            nc.scalar.mul(neg_gain[:], gain_shift_t[:, 0:OUT_TILES], -1.0)
-
-        stats = keep.tile([P, OUT_TILES, len(BANK_STARTS), BN_STATS_DIM], F32)
+        stats = keep.tile([P, OUT_TILES, len(BANK_STARTS) * BN_STATS_DIM], F32)
+        nc.gpsimd.memset(stats[:], float(BANK))
+        unread = keep.tile([P, BANK], BF16)
         mean_var = keep.tile([P, OUT_TILES, BN_AGGR_DIM], F32)
         neg_gain_mean = keep.tile([P, OUT_TILES], F32)
         inv_std = keep.tile([P, OUT_TILES], F32)
@@ -255,36 +262,65 @@ def tile_memory_sup_pb_kernel(
         out_view = out.rearrange("b (o p) h w -> o p b (h w)", p=P)
 
         with tc.psum_pool(name="acc", bufs=8, reuse_waits="tile") as acc:
+            y = {}
 
-            def statistics(o):
-                y_banks = []
-                for i, first in enumerate(BANK_STARTS):
-                    width = min(BANK, PIXELS - first)
-                    n_pass = BANK if width == BANK else P
-                    y = acc.tile([P, BANK], F32, tag="y")
-                    y_banks.append(y)
-                    for n0 in range(0, width, n_pass):
-                        cols = slice(first + n0, first + n0 + n_pass)
-                        for g in range(PASSES):
-                            nc.tensor.matmul_mx(
-                                out=y[:, n0 : n0 + n_pass],
-                                lhsT=w_words[:, g, 2 * P * o : 2 * P * (o + 1)].bitcast(FP4X4),
-                                lhsT_scale=w_scales[:, g, P * o : P * (o + 1)],
-                                rhs=upd_codes[:, g, cols].bitcast(FP8X4),
-                                rhs_scale=upd_scales[:, g, cols],
-                                start=(g == 0),
-                                stop=(g == PASSES - 1),
-                            )
-                    nc.vector.bn_stats(out=stats[:, o, i, :], in_=y[:, 0:width])
+            def pixels(i):
+                return slice(BANK_STARTS[i], min(BANK_STARTS[i] + BANK, PIXELS))
+
+            banks = {}
+            for first_of in BANK_ORDER:
+                bank = acc.tile([P, BANK], F32, tag="y")
+                banks[first_of] = bank
+
+            def multiply(o, i):
+                first, last = pixels(i).start, pixels(i).stop
+                n_pass = BANK if last - first == BANK else P
+                if (o, i) in banks:
+                    bank = banks[o, i]
+                else:
+                    bank = acc.tile([P, BANK], F32, tag="y")
+                for n0 in range(0, last - first, n_pass):
+                    cols = slice(first + n0, first + n0 + n_pass)
+                    for g in range(PASSES):
+                        nc.tensor.matmul_mx(
+                            out=bank[:, n0 : n0 + n_pass],
+                            lhsT=w_words[:, g, 2 * P * o : 2 * P * (o + 1)].bitcast(FP4X4),
+                            lhsT_scale=w_scales[:, g, P * o : P * (o + 1)],
+                            rhs=upd_codes[:, g, cols].bitcast(FP8X4),
+                            rhs_scale=upd_scales[:, g, cols],
+                            start=(g == 0),
+                            stop=(g == PASSES - 1),
+                        )
+                y[o, i] = bank[:, 0 : last - first]
+
+            def stats_at(o, i):
+                return sum(TRIPLE if (o, k) in SCALAR_STATS else BN_STATS_DIM for k in range(i))
+
+            def vector_stats(o, i):
+                at = stats_at(o, i)
+                nc.vector.bn_stats(out=stats[:, o, at : at + BN_STATS_DIM], in_=y[o, i])
+
+            def scalar_stats(o, i):
+                at = stats_at(o, i)
+                mean = stats[:, o, at + 1 : at + 2]
+                nc.scalar.activation(
+                    out=unread[:], in_=y[o, i], func=ACT.Identity, scale=1.0 / BANK, accum_out=mean
+                )
+                nc.scalar.activation(
+                    out=unread[:],
+                    in_=y[o, i],
+                    func=ACT.Square,
+                    scale=-1.0,
+                    bias=mean,
+                    accum_out=stats[:, o, at + 2 : at + 3],
+                )
+
+            def aggregate(o):
                 nc.vector.bn_aggr(
-                    out=mean_var[:, o, :], in_=stats[:, o].rearrange("p i s -> p (i s)")
+                    out=mean_var[:, o, :], in_=stats[:, o, 0 : stats_at(o, len(BANK_STARTS))]
                 )
-                nc.gpsimd.tensor_mul(
-                    neg_gain_mean[:, o : o + 1], mean_var[:, o, 0:1], neg_gain[:, o : o + 1]
-                )
-                return y_banks
 
-            def finish(o, y_banks):
+            def inverse_std(o):
                 one = slice(o, o + 1)
                 nc.scalar.activation(
                     out=inv_std[:, one],
@@ -292,6 +328,15 @@ def tile_memory_sup_pb_kernel(
                     func=ACT.Abs_reciprocal_sqrt,
                     bias=BN_EPS,
                 )
+                nc.scalar.activation(
+                    out=neg_gain_mean[:, one],
+                    in_=mean_var[:, o, 0:1],
+                    func=ACT.Copy,
+                    scale=neg_gain[:, one],
+                )
+
+            def scale_shift(o):
+                one = slice(o, o + 1)
                 nc.scalar.activation(
                     out=scale[:, one], in_=gain_shift[:, one], func=ACT.Copy, scale=inv_std[:, one]
                 )
@@ -302,33 +347,79 @@ def tile_memory_sup_pb_kernel(
                     scale=inv_std[:, one],
                     bias=gain_shift[:, OUT_TILES + o : OUT_TILES + o + 1],
                 )
-                result = stage.tile([P, PIXELS], F32, bufs=OUT_TILES)
-                for i, first in enumerate(BANK_STARTS):
-                    width = min(BANK, PIXELS - first)
-                    y = y_banks[i][:, 0:width]
-                    res = result[:, first : first + width]
-                    if o >= OUT_TILES - 2 and i == 1:
-                        nc.vector.tensor_scalar(
-                            out=res,
-                            in0=y,
-                            scalar1=scale[:, one],
-                            scalar2=shift[:, one],
-                            op0=ALU.mult,
-                            op1=ALU.add,
-                        )
-                        nc.vector.tensor_scalar_max(res, res, 0.0)
-                    else:
-                        nc.scalar.activation(
-                            out=res, in_=y, func=ACT.Relu, scale=scale[:, one], bias=shift[:, one]
-                        )
-                    nc.sync.dma_start(
-                        out=out_view[o][:, first // HW : (first + width) // HW, :],
-                        in_=res.rearrange("p (b n) -> p b n", n=HW),
-                    )
 
-            y_of = {}
-            for o in range(OUT_TILES + 1):
-                if o < OUT_TILES:
-                    y_of[o] = statistics(o)
-                if o > 0:
-                    finish(o - 1, y_of[o - 1])
+            def finish(o, i):
+                one = slice(o, o + 1)
+                first, last = pixels(i).start, pixels(i).stop
+                result = stage.tile([P, BANK], F32, bufs=len(BANK_STARTS) * OUT_TILES)
+                res = result[:, 0 : last - first]
+                if (o, i) in VECTOR_FINISHES:
+                    nc.vector.tensor_scalar(
+                        out=res,
+                        in0=y[o, i],
+                        scalar1=scale[:, one],
+                        scalar2=shift[:, one],
+                        op0=ALU.mult,
+                        op1=ALU.add,
+                    )
+                    nc.vector.tensor_scalar_max(res, res, 0.0)
+                else:
+                    nc.scalar.activation(
+                        out=res,
+                        in_=y[o, i],
+                        func=ACT.Relu,
+                        scale=scale[:, one],
+                        bias=shift[:, one],
+                    )
+                nc.sync.dma_start(
+                    out=out_view[o][:, first // HW : last // HW, :],
+                    in_=res.rearrange("p (b n) -> p b n", n=HW),
+                )
+
+            multiply(0, 0)
+            scalar_stats(0, 0)
+            multiply(0, 1)
+            multiply(0, 2)
+            multiply(1, 0)
+            for i in range(3):
+                if (0, i) not in SCALAR_STATS:
+                    vector_stats(0, i)
+            aggregate(0)
+            multiply(1, 1)
+            multiply(1, 2)
+            for i in range(3):
+                if (1, i) not in SCALAR_STATS:
+                    vector_stats(1, i)
+            aggregate(1)
+            inverse_std(0)
+            scale_shift(0)
+            multiply(2, 0)
+            multiply(2, 1)
+            finish(0, 0)
+            finish(0, 1)
+            inverse_std(1)
+            finish(0, 2)
+            scale_shift(1)
+            multiply(2, 2)
+            for i in range(3):
+                vector_stats(2, i)
+            aggregate(2)
+            multiply(3, 0)
+            multiply(3, 1)
+            finish(1, 0)
+            finish(1, 1)
+            inverse_std(2)
+            finish(1, 2)
+            scale_shift(2)
+            multiply(3, 2)
+            for i in range(3):
+                vector_stats(3, i)
+            aggregate(3)
+            finish(2, 0)
+            finish(2, 2)
+            inverse_std(3)
+            finish(2, 1)
+            scale_shift(3)
+            finish(3, 0)
+            finish(3, 1)
+            finish(3, 2)

from contextlib import ExitStack

import concourse.mybir as mybir
from concourse.masks import make_identity

F32 = mybir.dt.float32
BF16 = mybir.dt.bfloat16
I32 = mybir.dt.int32
U32 = mybir.dt.uint32
U8 = mybir.dt.uint8
FP8X4 = mybir.dt.float8_e4m3fn_x4
FP4X4 = mybir.dt.float4_e2m1fn_x4
ACT = mybir.ActivationFunctionType
ALU = mybir.AluOpType

P = 128
PACK = 4
BATCH = 5
CHANNELS = 512
HW = 256
PIXELS = BATCH * HW
OUT_CHANNELS = 512
OUT_TILES = OUT_CHANNELS // P
PASSES = 2
HALVES = HW // P
BANK = 512
BANK_STARTS = tuple(range(0, PIXELS, BANK))
L2_EPS = 1e-12
BN_EPS = 1e-5
BN_STATS_DIM = 6
BN_AGGR_DIM = 2
TRIPLE = BN_STATS_DIM // 2
BANK_ORDER = ((0, 0), (0, 1), (0, 2), (1, 0), (1, 1), (1, 2), (2, 0), (2, 1))
SCALAR_STATS = ((0, 0),)
VECTOR_FINISHES = ((2, 1), (3, 1))
CM_CHUNKS_ON_VECTOR = 1

FLOPS = 2 * PIXELS * PASSES * CHANNELS * OUT_CHANNELS


def tile_memory_sup_pb_kernel(
    tc, query, concat_memory, conv_w_words, conv_w_scales, bn_gamma, bn_beta, out
):
    nc = tc.nc
    with ExitStack() as ctx:
        ctx.enter_context(tc.manual_schedule())
        keep = ctx.enter_context(tc.tile_pool(name="keep", bufs=1))
        stage = ctx.enter_context(tc.tile_pool(name="stage", bufs=3))

        gain_shift_rows = keep.tile([P, P], BF16)
        nc.vector.memset(gain_shift_rows[:], 0.0)
        nc.scalar.dma_start(
            out=gain_shift_rows[0:OUT_TILES, :], in_=bn_gamma.rearrange("(j p) -> j p", p=P)
        )
        nc.scalar.dma_start(
            out=gain_shift_rows[OUT_TILES : 2 * OUT_TILES, :],
            in_=bn_beta.rearrange("(j p) -> j p", p=P),
        )

        one_column = keep.tile([P, 1], F32)
        nc.vector.memset(one_column[:], 1.0)
        table_warm = keep.tile([P, 1], F32)
        nc.scalar.activation(
            out=table_warm[:], in_=one_column[:], func=ACT.Abs_reciprocal_sqrt
        )

        ident_bf = keep.tile([P, P], BF16)
        make_identity(nc, ident_bf[:])
        beside = keep.tile([P, P], BF16)
        nc.gpsimd.tensor_scalar(
            out=beside[:], in0=ident_bf[:], scalar1=-1.0, scalar2=2.0**120, op0=ALU.add, op1=ALU.mult
        )
        ident_f32 = keep.tile([P, P], F32)
        make_identity(nc, ident_f32[:])

        w_scales = keep.tile([P, PASSES, OUT_CHANNELS], U8, align_bytes=64)
        nc.vector.memset(w_scales[:].bitcast(I32), 0)

        q_sb = keep.tile([P, BATCH, PACK, HW], BF16)
        cm_sb = keep.tile([P, BATCH, HALVES, CHANNELS], BF16)

        def load_query(b):
            nc.sync.dma_start(
                out=q_sb[:, b], in_=query[b].rearrange("(p t) h w -> p t (h w)", t=PACK)
            )

        def load_memory(c):
            nc.sync.dma_start(
                out=cm_sb[:, c],
                in_=concat_memory[HW * c : HW * (c + 1), :].rearrange(
                    "(r j) k -> r j k", j=HALVES
                ),
            )

        load_query(0)
        load_memory(0)
        load_query(1)
        load_query(2)
        load_memory(1)
        load_query(3)
        load_query(4)
        for c in range(2, BATCH):
            load_memory(c)
        w_words = keep.tile([P, PASSES, 2 * OUT_CHANNELS], U8, align_bytes=64)
        nc.sync.dma_start(
            out=w_words[:].bitcast(I32),
            in_=conv_w_words.bitcast(I32).rearrange("g p n -> p g n"),
        )
        for quadrant in range(4):
            nc.sync.dma_start(
                out=w_scales[32 * quadrant : 32 * quadrant + 4].bitcast(I32),
                in_=conv_w_scales.bitcast(I32)[:, 4 * quadrant : 4 * quadrant + 4, :].rearrange(
                    "g r n -> r g n"
                ),
            )

        upd_codes = keep.tile([P, PASSES, PIXELS], U32, align_bytes=64)
        upd_scales = keep.tile([P, PASSES, PIXELS], U8, align_bytes=64)

        squares = keep.tile([P, BATCH * HALVES, CHANNELS], BF16)
        sum_sq = keep.tile([P, BATCH * HALVES], F32)
        inv_norm = keep.tile([P, BATCH * HALVES], F32)
        gain_shift = keep.tile([P, 2 * OUT_TILES], F32)
        neg_gain = keep.tile([P, OUT_TILES], F32)

        with tc.psum_pool(name="prep", bufs=1) as prep:

            def inverse_norms(b):
                tiles_b = slice(HALVES * b, HALVES * (b + 1))
                nc.scalar.activation(
                    out=inv_norm[:, tiles_b],
                    in_=sum_sq[:, tiles_b],
                    func=ACT.Abs_reciprocal_sqrt,
                    bias=L2_EPS * L2_EPS,
                )

            def norms(b):
                for h in range(HALVES):
                    j = HALVES * b + h
                    q_t = prep.tile([P, PACK, P], BF16, tag="q_t", bufs=4)
                    for t in range(PACK):
                        nc.tensor.transpose(
                            q_t[:, t, :], q_sb[:, b, t, P * h : P * (h + 1)], ident_bf[:]
                        )
                    nc.scalar.activation(
                        out=squares[:, j, :],
                        in_=q_t[:].rearrange("n t p -> n (t p)"),
                        func=ACT.Square,
                        accum_out=sum_sq[:, j : j + 1],
                    )
                tiles_b = slice(HALVES * b, HALVES * (b + 1))
                nc.scalar.activation(
                    out=sum_sq[:, tiles_b],
                    in_=sum_sq[:, tiles_b],
                    func=ACT.Relu,
                    bias=-L2_EPS * L2_EPS,
                )
                inverse_norms(b)

            def normalise(b):
                inv_norm_all = prep.tile([P, HW], F32, tag="inv_norm_all", bufs=2)
                for h in range(HALVES):
                    j = HALVES * b + h
                    nc.tensor.transpose(
                        inv_norm_all[:, P * h : P * (h + 1)],
                        inv_norm[:, j : j + 1].to_broadcast([P, P]),
                        ident_f32[:],
                    )
                q_grouped = stage.tile([P, HW, PACK], BF16, align_bytes=64)
                nc.vector.tensor_mul(
                    q_grouped[:],
                    inv_norm_all[:].unsqueeze(2).to_broadcast([P, HW, PACK]),
                    q_sb[:, b].rearrange("p t n -> p n t"),
                )
                return q_grouped[:].rearrange("p n t -> p (n t)")

            def memory_words(c):
                cm_t = prep.tile([P, HALVES, 2, P], F32, tag="cm_t", bufs=2)
                for j in range(HALVES):
                    cm_words = cm_sb[:, c, j, :].bitcast(F32)
                    for u in range(2):
                        nc.tensor.transpose(
                            cm_t[:, j, u, :], cm_words[:, u : CHANNELS // 2 : 2], ident_f32[:]
                        )
                cm_grouped = stage.tile([P, HW * 2], F32, align_bytes=64)
                side_by_side = cm_grouped[:].rearrange("p (r j u) -> p r j u", j=HALVES, u=2)
                if c < CM_CHUNKS_ON_VECTOR:
                    nc.vector.tensor_copy(out=side_by_side, in_=cm_t[:].rearrange("p j u r -> p r j u"))
                else:
                    nc.scalar.copy(out=side_by_side, in_=cm_t[:].rearrange("p j u r -> p r j u"))
                return cm_grouped[:].bitcast(BF16)

            def gains():
                gain_shift_t = prep.tile([P, P], BF16, tag="q_t", bufs=4)
                nc.tensor.transpose(gain_shift_t[:], gain_shift_rows[:], ident_bf[:])
                nc.scalar.copy(out=gain_shift[:], in_=gain_shift_t[:, 0 : 2 * OUT_TILES])
                nc.scalar.mul(neg_gain[:], gain_shift_t[:, 0:OUT_TILES], -1.0)

            def quantise(g, c, grouped):
                cols = slice(HW * c, HW * (c + 1))
                nc.vector.quantize_mx(
                    out=upd_codes[:, g, cols].bitcast(FP8X4),
                    scales=upd_scales[:, g, cols],
                    in_=grouped,
                )

            def product_norms(b):
                for h in range(HALVES):
                    j = HALVES * b + h
                    gram = prep.tile([P, P], F32, tag="q_t", bufs=4)
                    for t in range(PACK):
                        pixels = q_sb[:, b, t, P * h : P * (h + 1)]
                        nc.tensor.matmul(gram[:], lhsT=pixels, rhs=pixels, start=(t == 0), stop=False)
                    nc.tensor.matmul(
                        gram[:], lhsT=ident_bf[:], rhs=beside[:], start=False, stop=True
                    )
                    nc.scalar.activation(
                        out=squares[:, j, 0:P],
                        in_=gram[:],
                        func=ACT.Relu,
                        bias=-L2_EPS * L2_EPS,
                        accum_out=sum_sq[:, j : j + 1],
                    )
                inverse_norms(b)


            product_norms(0)
            m0 = memory_words(0)
            product_norms(1)
            quantise(1, 0, m0)
            q0 = normalise(0)
            product_norms(2)
            q1 = normalise(1)
            norms(3)
            quantise(0, 0, q0)
            m1 = memory_words(1)
            q2 = normalise(2)
            quantise(0, 1, q1)
            norms(4)
            quantise(1, 1, m1)
            q3 = normalise(3)
            m2 = memory_words(2)
            quantise(0, 2, q2)
            m3 = memory_words(3)
            gains()
            q4 = normalise(4)
            quantise(0, 3, q3)
            quantise(1, 2, m2)
            m4 = memory_words(4)
            quantise(1, 3, m3)
            quantise(0, 4, q4)
            quantise(1, 4, m4)

        stats = keep.tile([P, OUT_TILES, len(BANK_STARTS) * BN_STATS_DIM], F32)
        nc.gpsimd.memset(stats[:], float(BANK))
        unread = keep.tile([P, BANK], BF16)
        mean_var = keep.tile([P, OUT_TILES, BN_AGGR_DIM], F32)
        neg_gain_mean = keep.tile([P, OUT_TILES], F32)
        inv_std = keep.tile([P, OUT_TILES], F32)
        scale = keep.tile([P, OUT_TILES], F32)
        shift = keep.tile([P, OUT_TILES], F32)
        out_view = out.rearrange("b (o p) h w -> o p b (h w)", p=P)

        with tc.psum_pool(name="acc", bufs=8, reuse_waits="tile") as acc:
            y = {}

            def pixels(i):
                return slice(BANK_STARTS[i], min(BANK_STARTS[i] + BANK, PIXELS))

            banks = {}
            for first_of in BANK_ORDER:
                bank = acc.tile([P, BANK], F32, tag="y")
                banks[first_of] = bank

            def multiply(o, i):
                first, last = pixels(i).start, pixels(i).stop
                n_pass = BANK if last - first == BANK else P
                if (o, i) in banks:
                    bank = banks[o, i]
                else:
                    bank = acc.tile([P, BANK], F32, tag="y")
                for n0 in range(0, last - first, n_pass):
                    cols = slice(first + n0, first + n0 + n_pass)
                    for g in range(PASSES):
                        nc.tensor.matmul_mx(
                            out=bank[:, n0 : n0 + n_pass],
                            lhsT=w_words[:, g, 2 * P * o : 2 * P * (o + 1)].bitcast(FP4X4),
                            lhsT_scale=w_scales[:, g, P * o : P * (o + 1)],
                            rhs=upd_codes[:, g, cols].bitcast(FP8X4),
                            rhs_scale=upd_scales[:, g, cols],
                            start=(g == 0),
                            stop=(g == PASSES - 1),
                        )
                y[o, i] = bank[:, 0 : last - first]

            def stats_at(o, i):
                return sum(TRIPLE if (o, k) in SCALAR_STATS else BN_STATS_DIM for k in range(i))

            def vector_stats(o, i):
                at = stats_at(o, i)
                nc.vector.bn_stats(out=stats[:, o, at : at + BN_STATS_DIM], in_=y[o, i])

            def scalar_stats(o, i):
                at = stats_at(o, i)
                mean = stats[:, o, at + 1 : at + 2]
                nc.scalar.activation(
                    out=unread[:], in_=y[o, i], func=ACT.Identity, scale=1.0 / BANK, accum_out=mean
                )
                nc.scalar.activation(
                    out=unread[:],
                    in_=y[o, i],
                    func=ACT.Square,
                    scale=-1.0,
                    bias=mean,
                    accum_out=stats[:, o, at + 2 : at + 3],
                )

            def aggregate(o):
                nc.vector.bn_aggr(
                    out=mean_var[:, o, :], in_=stats[:, o, 0 : stats_at(o, len(BANK_STARTS))]
                )

            def inverse_std(o):
                one = slice(o, o + 1)
                nc.scalar.activation(
                    out=inv_std[:, one],
                    in_=mean_var[:, o, 1:2],
                    func=ACT.Abs_reciprocal_sqrt,
                    bias=BN_EPS,
                )
                nc.scalar.activation(
                    out=neg_gain_mean[:, one],
                    in_=mean_var[:, o, 0:1],
                    func=ACT.Copy,
                    scale=neg_gain[:, one],
                )

            def scale_shift(o):
                one = slice(o, o + 1)
                nc.scalar.activation(
                    out=scale[:, one], in_=gain_shift[:, one], func=ACT.Copy, scale=inv_std[:, one]
                )
                nc.scalar.activation(
                    out=shift[:, one],
                    in_=neg_gain_mean[:, one],
                    func=ACT.Identity,
                    scale=inv_std[:, one],
                    bias=gain_shift[:, OUT_TILES + o : OUT_TILES + o + 1],
                )

            def finish(o, i):
                one = slice(o, o + 1)
                first, last = pixels(i).start, pixels(i).stop
                result = stage.tile([P, BANK], F32, bufs=len(BANK_STARTS) * OUT_TILES)
                res = result[:, 0 : last - first]
                if (o, i) in VECTOR_FINISHES:
                    nc.vector.tensor_scalar(
                        out=res,
                        in0=y[o, i],
                        scalar1=scale[:, one],
                        scalar2=shift[:, one],
                        op0=ALU.mult,
                        op1=ALU.add,
                    )
                    nc.vector.tensor_scalar_max(res, res, 0.0)
                else:
                    nc.scalar.activation(
                        out=res,
                        in_=y[o, i],
                        func=ACT.Relu,
                        scale=scale[:, one],
                        bias=shift[:, one],
                    )
                nc.sync.dma_start(
                    out=out_view[o][:, first // HW : last // HW, :],
                    in_=res.rearrange("p (b n) -> p b n", n=HW),
                )

            multiply(0, 0)
            scalar_stats(0, 0)
            multiply(0, 1)
            multiply(0, 2)
            multiply(1, 0)
            for i in range(3):
                if (0, i) not in SCALAR_STATS:
                    vector_stats(0, i)
            aggregate(0)
            multiply(1, 1)
            multiply(1, 2)
            for i in range(3):
                if (1, i) not in SCALAR_STATS:
                    vector_stats(1, i)
            aggregate(1)
            inverse_std(0)
            scale_shift(0)
            multiply(2, 0)
            multiply(2, 1)
            finish(0, 0)
            finish(0, 1)
            inverse_std(1)
            finish(0, 2)
            scale_shift(1)
            multiply(2, 2)
            for i in range(3):
                vector_stats(2, i)
            aggregate(2)
            multiply(3, 0)
            multiply(3, 1)
            finish(1, 0)
            finish(1, 1)
            inverse_std(2)
            finish(1, 2)
            scale_shift(2)
            multiply(3, 2)
            for i in range(3):
                vector_stats(3, i)
            aggregate(3)
            finish(2, 0)
            finish(2, 2)
            inverse_std(3)
            finish(2, 1)
            scale_shift(3)
            finish(3, 0)
            finish(3, 1)
            finish(3, 2)
